import numpy as np
import ml_dtypes


def mxq(x, axis, fmt="e4m3"):
    dtype, down = {"e4m3": (ml_dtypes.float8_e4m3fn, 7), "e5m2": (ml_dtypes.float8_e5m2, 14)}[fmt]
    v = np.moveaxis(np.asarray(x, np.float32).astype(ml_dtypes.bfloat16).astype(np.float64), axis, -1)
    blocks = v.reshape(v.shape[:-1] + (-1, 32))
    amax = np.abs(blocks).max(-1, keepdims=True)
    byte = np.maximum(np.where(amax > 0, np.frexp(amax)[1] - 1 + 127, 0) - down, 1)
    scale = np.exp2(byte - 127.0)
    codes = (blocks / scale).astype(np.float32).astype(dtype).astype(np.float64)
    return np.moveaxis((codes * scale).reshape(v.shape), -1, axis)


WIDE = False


def mx_kscale(k):
    if not WIDE:
        return np.ones(k)
    levels = np.array([10, -10, 5, -5, 0])
    a = np.random.permutation(np.resize(levels, k // 512 * 4)).reshape(k // 512, 4)
    idx = np.arange(k)
    return np.exp2(a[idx // 512, idx % 128 // 32])


BF16 = ml_dtypes.bfloat16


def bf(x):
    return np.asarray(x, np.float32).astype(BF16)


def f64(x):
    return np.asarray(x).astype(np.float64)


B, Nx, Nh, Ny, G = 8192, 1024, 512, 256, 4
NU = 1.0


def setup_inputs():
    s = mx_kscale(Nx)
    base = np.random.standard_normal((G, Nx))
    w = np.random.standard_normal((Nh, Nx)) * np.sqrt(24.0 / (Nx * Nh))
    b = np.random.standard_normal(Nh) * 2.0 / np.sqrt(Nh)
    hid = np.stack([np.maximum((w * np.maximum(base[g], 0.0)).sum(axis=1) + b, 0.0) for g in range(G)])
    x = np.sqrt(0.75) * base[np.random.randint(0, G, B)] + 0.5 * np.random.standard_normal((B, Nx))
    wq = np.random.uniform(0.5, 1.5, (Ny, 1)) * hid[np.random.randint(0, G, Ny)] + np.random.standard_normal((Ny, Nh)) / np.sqrt(Nh)
    return {"x": bf(x * s),
            "W_fc": bf(w / s[None, :]),
            "b_fc": bf(b),
            "W_q": bf(wq)}


def reference(x, W_fc, b_fc, W_q):
    wq = f64(W_q)
    a = np.maximum(f64(x), 0.0)
    h = np.maximum((mxq(a, 1, "e4m3") @ mxq(f64(W_fc), 1, "e4m3").T) + f64(b_fc), 0.0)
    d = (np.sum(h * h, axis=-1, keepdims=True)
         - 2.0 * (mxq(h, 1, "e4m3") @ mxq(wq, 1, "e4m3").T)
         + np.sum(wq * wq, axis=-1))
    d = np.maximum(d, 0.0)
    t = (-(NU + 1.0) / 2.0) * np.log1p(d / NU)
    m = t.max(axis=-1, keepdims=True)
    return t - (m + np.log(np.sum(np.exp(t - m), axis=-1, keepdims=True)))

@@ -1,0 +1,340 @@
+from contextlib import ExitStack
+
+import concourse.mybir as mybir
+from concourse.masks import make_identity
+
+F32 = mybir.dt.float32
+BF16 = mybir.dt.bfloat16
+U32 = mybir.dt.uint32
+U8 = mybir.dt.uint8
+FP8X4 = mybir.dt.float8_e4m3fn_x4
+ACT = mybir.ActivationFunctionType
+ALU = mybir.AluOpType
+
+P = 128
+B, NX, NH, NY = 8192, 1024, 512, 256
+BLK = 512
+NB = B // BLK
+T = BLK // P
+FLOPS = 2 * B * NX * NH + 2 * B * NH * NY
+
+MANUAL = True
+GROUPS = [[0, 1, 2, 3], [4, 5, 6, 7], [8, 9, 10, 11], [12, 13, 14], [15]]
+SLICES_PER_QUARTER = 3
+FIN_PER_QUARTER = 2
+V1_ON_GPSIMD = True
+FIN_V_GROUPS = (3, 4)
+X_BUFS = 4
+
+
+def s1_on_vector(k, m):
+    return k >= 4 and m in (1, 3)
+
+
+def tile_tnet_t_kernel(tc, x, W_fc, b_fc, W_q, out):
+    nc = tc.nc
+    with ExitStack() as ctx:
+        const = ctx.enter_context(tc.tile_pool(name="const", bufs=1))
+        xpool = ctx.enter_context(tc.tile_pool(name="xpool", bufs=X_BUFS))
+        apool = ctx.enter_context(tc.tile_pool(name="apool", bufs=2))
+        hpool = ctx.enter_context(tc.tile_pool(name="hpool", bufs=3))
+        gpool = ctx.enter_context(tc.tile_pool(name="gpool", bufs=2))
+        ps_x = ctx.enter_context(tc.psum_pool(name="ps_x", bufs=2))
+        ps_h = ctx.enter_context(tc.psum_pool(name="ps_h", bufs=2))
+        ps_z = ctx.enter_context(tc.psum_pool(name="ps_z", bufs=2))
+        ps_g = ctx.enter_context(tc.psum_pool(name="ps_g", bufs=2))
+        if MANUAL:
+            ctx.enter_context(tc.manual_schedule())
+
+        ident = const.tile([P, P], F32, name="ident")
+        wfc_sb = const.tile([P, 4, NX], BF16, name="wfc_sb")
+        wg = const.tile([P, 2 * NH * 4], BF16, name="wg", align_bytes=64)
+        wfc_codes = const.tile([P, 2, NH], U32, name="wfc_codes", align_bytes=64)
+        wfc_scales = const.tile([P, 2, NH], U8, name="wfc_scales", align_bytes=64)
+        b_bf = const.tile([P, 4], BF16, name="b_bf")
+        bias = const.tile([P, 4], F32, name="bias")
+        wq_sb = const.tile([P, 2, NH], BF16, name="wq_sb")
+        wqg = const.tile([P, NY * 4], BF16, name="wqg", align_bytes=64)
+        wq_codes = const.tile([P, NY], U32, name="wq_codes", align_bytes=64)
+        wq_scales = const.tile([P, NY], U8, name="wq_scales", align_bytes=64)
+        ww = const.tile([P, 2], F32, name="ww")
+        wwb1 = const.tile([P, NY], F32, name="wwb1")
+        junk_sq = const.tile([P, NH], BF16, name="junk_sq")
+        junk_ex = const.tile([P, NY], BF16, name="junk_ex")
+        hh = const.tile([P, NB * T], F32, name="hh")
+        umin = const.tile([P, NB * T], F32, name="umin")
+        rmin = const.tile([P, NB * T], F32, name="rmin")
+        ssum = const.tile([P, NB * T], F32, name="ssum")
+        lns = const.tile([P, NB * T], F32, name="lns")
+        u_tiles = [const.tile([P, T, NY], F32, name="u%d" % i) for i in range(NB)]
+
+        xs = {}
+        ag = {}
+        a_codes = {}
+        a_scales = {}
+        h32 = {}
+        h_codes = {}
+        h_scales = {}
+
+        def load(i):
+            xs[i] = xpool.tile([P, T, NX], BF16, name="x%d" % i, tag="x")
+            nc.sync.dma_start(
+                out=xs[i][:],
+                in_=x[i * BLK:(i + 1) * BLK, :].rearrange("(p t) k -> p t k", t=T),
+            )
+
+        def setup_wfc():
+            for m in range(4):
+                wt = ps_x.tile([P, 512], F32, name="wt%d" % m, tag="xt")
+                words = wfc_sb[:, m, :].bitcast(F32)
+                for gu in range(4):
+                    nc.tensor.transpose(
+                        wt[:, gu * P:(gu + 1) * P], words[:, gu * P:(gu + 1) * P], ident[:]
+                    )
+                dst = wg[:].bitcast(F32).rearrange("p (g c u) -> p g c u", g=2, u=2)
+                dst = dst[:, :, m * P:(m + 1) * P, :]
+                src = wt[:].rearrange("p (g u n) -> p g n u", g=2, u=2)
+                if m % 2 == 0:
+                    nc.vector.tensor_copy(out=dst, in_=src)
+                else:
+                    nc.scalar.copy(out=dst, in_=src)
+            for g in range(2):
+                nc.vector.quantize_mx(
+                    out=wfc_codes[:, g, :].bitcast(FP8X4),
+                    scales=wfc_scales[:, g, :],
+                    in_=wg[:, g * NH * 4:(g + 1) * NH * 4],
+                )
+            nc.vector.tensor_copy(out=bias[:], in_=b_bf[:])
+
+        def setup_wq():
+            for c in range(2):
+                nc.scalar.activation(
+                    out=junk_sq[:], in_=wq_sb[:, c, :], func=ACT.Square,
+                    accum_out=ww[:, c:c + 1],
+                )
+            wwps = ps_g.tile([P, NY], F32, name="wwps", tag="g")
+            for c in range(2):
+                rep = const.tile([P, P], F32, name="rep%d" % c)
+                nc.vector.tensor_copy(out=rep[:], in_=ww[:, c:c + 1].to_broadcast([P, P]))
+                nc.tensor.transpose(wwps[:, c * P:(c + 1) * P], rep[:], ident[:])
+            nc.vector.tensor_scalar(
+                out=wwb1[:], in0=wwps[:], scalar1=1.0, scalar2=None, op0=ALU.add
+            )
+            wqt = ps_h.tile([P, 512], F32, name="wqt", tag="ht")
+            for c in range(2):
+                words = wq_sb[:, c, :].bitcast(F32).rearrange("j (p u) -> j u p", u=2)
+                for u in range(2):
+                    nc.tensor.transpose(
+                        wqt[:, u * NY + c * P:u * NY + (c + 1) * P], words[:, u, :], ident[:]
+                    )
+            nc.vector.tensor_scalar(
+                out=wqg[:].rearrange("p (j u e) -> p j u e", u=2, e=2),
+                in0=wqt[:].bitcast(BF16).rearrange("p (u j e) -> p j u e", u=2, e=2),
+                scalar1=-2.0, scalar2=None, op0=ALU.mult,
+            )
+            nc.vector.quantize_mx(
+                out=wq_codes[:].bitcast(FP8X4), scales=wq_scales[:], in_=wqg[:]
+            )
+
+        def stage_xt(i, t):
+            if t == 0:
+                ag[i] = apool.tile([P, 2, BLK, 4], BF16, name="ag%d" % i, tag="ag", align_bytes=64)
+                a_codes[i] = apool.tile([P, 2, BLK], U32, name="ac%d" % i, tag="ac", align_bytes=64)
+                a_scales[i] = apool.tile([P, 2, BLK], U8, name="as%d" % i, tag="as", align_bytes=64)
+            xt = ps_x.tile([P, 512], F32, name="xt%d_%d" % (i, t), tag="xt")
+            words = xs[i][:, t, :].bitcast(F32)
+            for gu in range(4):
+                nc.tensor.transpose(
+                    xt[:, gu * P:(gu + 1) * P], words[:, gu * P:(gu + 1) * P], ident[:]
+                )
+            pairs = xt[:].bitcast(BF16).rearrange("p (g u r e) -> p g r u e", g=2, u=2, e=2)
+            for g in range(2):
+                nc.vector.tensor_scalar(
+                    out=ag[i][:, g, t * P:(t + 1) * P, :].rearrange("p r (u e) -> p r u e", u=2),
+                    in0=pairs[:, g],
+                    scalar1=0.0, scalar2=None, op0=ALU.max,
+                )
+
+        def stage_qa(i, t):
+            for g in range(2):
+                nc.vector.quantize_mx(
+                    out=a_codes[i][:, g, t * P:(t + 1) * P].bitcast(FP8X4),
+                    scales=a_scales[i][:, g, t * P:(t + 1) * P],
+                    in_=ag[i][:, g, t * P:(t + 1) * P, :].rearrange("p r f -> p (r f)"),
+                )
+
+        def stage_l1(i, m):
+            if m == 0:
+                h32[i] = hpool.tile([P, 4, BLK], F32, name="h32_%d" % i, tag="h32")
+            z = ps_z.tile([P, BLK], F32, name="z%d_%d" % (i, m), tag="z")
+            for g in range(2):
+                nc.tensor.matmul_mx(
+                    out=z[:],
+                    lhsT=wfc_codes[:, g, m * P:(m + 1) * P].bitcast(FP8X4),
+                    lhsT_scale=wfc_scales[:, g, m * P:(m + 1) * P],
+                    rhs=a_codes[i][:, g, :].bitcast(FP8X4),
+                    rhs_scale=a_scales[i][:, g, :],
+                    start=(g == 0), stop=(g == 1),
+                )
+            if s1_on_vector(i, m):
+                nc.vector.tensor_scalar(
+                    out=h32[i][:, m, :], in0=z[:], scalar1=bias[:, m:m + 1], scalar2=0.0,
+                    op0=ALU.add, op1=ALU.max,
+                )
+            else:
+                nc.scalar.activation(
+                    out=h32[i][:, m, :], in_=z[:], func=ACT.Relu, bias=bias[:, m:m + 1], scale=1.0
+                )
+
+        hg = {}
+
+        def stage_v1(i):
+            hg[i] = gpool.tile([P, BLK, 4], BF16, name="hg%d" % i, tag="hg", align_bytes=64)
+            src = h32[i][:].rearrange("p m b -> p b m")
+            if V1_ON_GPSIMD:
+                nc.gpsimd.tensor_scalar(
+                    out=hg[i][:], in0=src, scalar1=1.0, scalar2=0.0, op0=ALU.mult, op1=ALU.add
+                )
+            else:
+                nc.vector.tensor_copy(out=hg[i][:], in_=src)
+
+        def stage_qh(i):
+            h_codes[i] = hpool.tile([P, BLK], U32, name="hc%d" % i, tag="hc", align_bytes=64)
+            h_scales[i] = hpool.tile([P, BLK], U8, name="hs%d" % i, tag="hs", align_bytes=64)
+            nc.vector.quantize_mx(
+                out=h_codes[i][:].bitcast(FP8X4), scales=h_scales[i][:],
+                in_=hg[i][:].rearrange("p b m -> p (b m)"),
+            )
+
+        def stage_ht(i, t):
+            ht = ps_h.tile([P, 512], F32, name="ht%d_%d" % (i, t), tag="ht")
+            for m in range(4):
+                nc.tensor.transpose(
+                    ht[:, m * P:(m + 1) * P], h32[i][:, m, t * P:(t + 1) * P], ident[:]
+                )
+            col = i * T + t
+            nc.scalar.activation(
+                out=junk_sq[:], in_=ht[:], func=ACT.Square, accum_out=hh[:, col:col + 1]
+            )
+
+        def stage_l2(i, t):
+            col = i * T + t
+            gp = ps_g.tile([P, NY], F32, name="g%d_%d" % (i, t), tag="g")
+            nc.tensor.matmul_mx(
+                out=gp[:],
+                lhsT=h_codes[i][:, t * P:(t + 1) * P].bitcast(FP8X4),
+                lhsT_scale=h_scales[i][:, t * P:(t + 1) * P],
+                rhs=wq_codes[:].bitcast(FP8X4),
+                rhs_scale=wq_scales[:],
+                start=True, stop=True,
+            )
+            u = u_tiles[i]
+            nc.vector.scalar_tensor_tensor(
+                out=u[:, t, :], in0=gp[:], scalar=hh[:, col:col + 1], in1=wwb1[:],
+                op0=ALU.add, op1=ALU.add,
+            )
+            nc.vector.tensor_scalar(
+                out=u[:, t, :], in0=u[:, t, :], scalar1=1.0, scalar2=None,
+                op0=ALU.max, op1=ALU.min, accum_out=umin[:, col:col + 1],
+            )
+            if t == T - 1:
+                nc.vector.reciprocal(out=rmin[:, i * T:(i + 1) * T], in_=umin[:, i * T:(i + 1) * T])
+
+        units = []
+        for q in range(len(GROUPS)):
+            if q > 0:
+                units.append(("LS", q - 1, 0))
+            for i in GROUPS[q]:
+                for t in range(T):
+                    units.append(("LN", i, t))
+            for i in GROUPS[q]:
+                for t in range(T):
+                    units.append(("EX", i, t))
+        units.append(("LS", len(GROUPS) - 1, 0))
+        state = {"unit": 0, "ready": -1, "fin": 0}
+        fins = []
+
+        def emit_units(limit):
+            n = 0
+            while state["unit"] < len(units) and n < limit:
+                kind, a, t = units[state["unit"]]
+                if kind != "LS" and a > state["ready"]:
+                    return
+                if kind == "LS":
+                    c0 = GROUPS[a][0] * T
+                    c1 = (GROUPS[a][-1] + 1) * T
+                    nc.scalar.activation(out=lns[:, c0:c1], in_=ssum[:, c0:c1], func=ACT.Ln)
+                    for i in GROUPS[a]:
+                        for tt in range(T):
+                            fins.append((a, i, tt))
+                else:
+                    col = a * T + t
+                    u = u_tiles[a]
+                    if kind == "LN":
+                        nc.scalar.activation(
+                            out=u[:, t, :], in_=u[:, t, :], func=ACT.Ln, scale=rmin[:, col:col + 1]
+                        )
+                    else:
+                        nc.scalar.activation(
+                            out=junk_ex[:], in_=u[:, t, :], func=ACT.Exp, scale=-1.0,
+                            accum_out=ssum[:, col:col + 1],
+                        )
+                state["unit"] += 1
+                n += 1
+
+        def emit_fins(limit):
+            n = 0
+            while state["fin"] < len(fins) and n < limit:
+                q, i, t = fins[state["fin"]]
+                col = i * T + t
+                u = u_tiles[i]
+                eng = nc.vector if q in FIN_V_GROUPS else nc.gpsimd
+                eng.tensor_scalar(
+                    out=u[:, t, :], in0=u[:, t, :], scalar1=lns[:, col:col + 1], scalar2=-1.0,
+                    op0=ALU.add, op1=ALU.mult,
+                )
+                if t == T - 1:
+                    nc.sync.dma_start(
+                        out=out[i * BLK:(i + 1) * BLK, :].rearrange("(p t) j -> p t j", t=T),
+                        in_=u[:],
+                    )
+                state["fin"] += 1
+                n += 1
+
+        nc.sync.dma_start(out=wfc_sb[:], in_=W_fc.rearrange("(p m) k -> p m k", m=4))
+        nc.scalar.dma_start(out=b_bf[:], in_=b_fc.rearrange("(p m) -> p m", m=4))
+        nc.scalar.dma_start(out=wq_sb[:], in_=W_q.rearrange("(c j) k -> j c k", c=2))
+        for i in range(X_BUFS):
+            load(i)
+        make_identity(nc, ident[:])
+        setup_wfc()
+
+        for k in range(-1, NB + 2):
+            for t in range(T):
+                if t == 0:
+                    if 0 <= k < NB:
+                        stage_qa(k, T - 1)
+                elif 0 <= k + 1 < NB:
+                    stage_qa(k + 1, t - 1)
+                if 0 <= k + 1 < NB:
+                    stage_xt(k + 1, t)
+                if 0 <= k - 1 < NB:
+                    if t == 0:
+                        stage_v1(k - 1)
+                    stage_ht(k - 1, t)
+                if 0 <= k < NB:
+                    stage_l1(k, t)
+                if 0 <= k - 2 < NB:
+                    stage_l2(k - 2, t)
+                    if t == T - 1:
+                        state["ready"] = k - 2
+                if t == 2 and 0 <= k - 1 < NB:
+                    stage_qh(k - 1)
+                emit_units(SLICES_PER_QUARTER)
+                emit_fins(FIN_PER_QUARTER)
+            if k == -1:
+                setup_wq()
+            if 0 <= k + 1 + X_BUFS < NB + 0 and k + 1 >= 0:
+                load(k + 1 + X_BUFS - 0)
+        emit_units(len(units))
+        emit_fins(len(fins))

@@ -16,19 +16,33 @@ B, NX, NH, NY = 8192, 1024, 512, 256
 BLK = 512
 NB = B // BLK
 T = BLK // P
+NT = NB * T
 FLOPS = 2 * B * NX * NH + 2 * B * NH * NY
 
-MANUAL = True
-GROUPS = [[0, 1, 2, 3], [4, 5, 6, 7], [8, 9, 10, 11], [12, 13, 14], [15]]
-SLICES_PER_QUARTER = 3
-FIN_PER_QUARTER = 2
-V1_ON_GPSIMD = True
-FIN_V_GROUPS = (3, 4)
+GROUPS = [[0,1,2,3],[4,5,6,7],[8,9,10,11],[12,13,14],[15]]
+UNITS_PER_STEP = 3
+FINS_PER_STEP = 2
+FIN_LAG = 2
+LN_LAG = 1
+DUMMY = 1
+V1_ON_GPSIMD = False
+HG_BUFS = 3
 X_BUFS = 4
+WQ_AT = 3
+LAG_XE = 1
+LAG_QA = 2
+LAG_L1 = 6
+LAG_S1 = 7
+LAG_V1 = 11
+LAG_HT = 11
+LAG_SQ = 12
+LAG_QH = 12
+LAG_L2 = 13
+LAG_E = 14
 
 
-def s1_on_vector(k, m):
-    return k >= 4 and m in (1, 3)
+def s1_on_vector(i, m):
+    return i >= 13 and m % 2 == 1
 
 
 def tile_tnet_t_kernel(tc, x, W_fc, b_fc, W_q, out):
@@ -36,15 +50,15 @@ def tile_tnet_t_kernel(tc, x, W_fc, b_fc, W_q, out):
     with ExitStack() as ctx:
         const = ctx.enter_context(tc.tile_pool(name="const", bufs=1))
         xpool = ctx.enter_context(tc.tile_pool(name="xpool", bufs=X_BUFS))
+        agpool = ctx.enter_context(tc.tile_pool(name="agpool", bufs=3))
         apool = ctx.enter_context(tc.tile_pool(name="apool", bufs=2))
         hpool = ctx.enter_context(tc.tile_pool(name="hpool", bufs=3))
-        gpool = ctx.enter_context(tc.tile_pool(name="gpool", bufs=2))
+        hgpool = ctx.enter_context(tc.tile_pool(name="hgpool", bufs=HG_BUFS))
         ps_x = ctx.enter_context(tc.psum_pool(name="ps_x", bufs=2))
         ps_h = ctx.enter_context(tc.psum_pool(name="ps_h", bufs=2))
         ps_z = ctx.enter_context(tc.psum_pool(name="ps_z", bufs=2))
         ps_g = ctx.enter_context(tc.psum_pool(name="ps_g", bufs=2))
-        if MANUAL:
-            ctx.enter_context(tc.manual_schedule())
+        ctx.enter_context(tc.manual_schedule())
 
         ident = const.tile([P, P], F32, name="ident")
         wfc_sb = const.tile([P, 4, NX], BF16, name="wfc_sb")
@@ -61,20 +75,26 @@ def tile_tnet_t_kernel(tc, x, W_fc, b_fc, W_q, out):
         wwb1 = const.tile([P, NY], F32, name="wwb1")
         junk_sq = const.tile([P, NH], BF16, name="junk_sq")
         junk_ex = const.tile([P, NY], BF16, name="junk_ex")
-        hh = const.tile([P, NB * T], F32, name="hh")
-        umin = const.tile([P, NB * T], F32, name="umin")
-        rmin = const.tile([P, NB * T], F32, name="rmin")
-        ssum = const.tile([P, NB * T], F32, name="ssum")
-        lns = const.tile([P, NB * T], F32, name="lns")
+        hh = const.tile([P, NT], F32, name="hh")
+        umin = const.tile([P, NT], F32, name="umin")
+        rmin = const.tile([P, NT], F32, name="rmin")
+        ssum = const.tile([P, NT], F32, name="ssum")
+        lns = const.tile([P, NT], F32, name="lns")
         u_tiles = [const.tile([P, T, NY], F32, name="u%d" % i) for i in range(NB)]
 
         xs = {}
-        ag = {}
+        xts = {}
+        agt = {}
         a_codes = {}
         a_scales = {}
+        zs = {}
         h32 = {}
+        hgp = {}
         h_codes = {}
         h_scales = {}
+        hts = {}
+        gps = {}
+        wq_tmp = {}
 
         def load(i):
             xs[i] = xpool.tile([P, T, NX], BF16, name="x%d" % i, tag="x")
@@ -106,120 +126,82 @@ def tile_tnet_t_kernel(tc, x, W_fc, b_fc, W_q, out):
                 )
             nc.vector.tensor_copy(out=bias[:], in_=b_bf[:])
 
-        def setup_wq():
-            for c in range(2):
-                nc.scalar.activation(
-                    out=junk_sq[:], in_=wq_sb[:, c, :], func=ACT.Square,
-                    accum_out=ww[:, c:c + 1],
+        def setup_wq(phase):
+            if phase == 0:
+                for c in range(2):
+                    nc.scalar.activation(
+                        out=junk_sq[:], in_=wq_sb[:, c, :], func=ACT.Square,
+                        accum_out=ww[:, c:c + 1],
+                    )
+                wqt = ps_h.tile([P, 512], F32, name="wqt", tag="ht")
+                wq_tmp["wqt"] = wqt
+                for c in range(2):
+                    words = wq_sb[:, c, :].bitcast(F32).rearrange("j (p u) -> j u p", u=2)
+                    for u in range(2):
+                        nc.tensor.transpose(
+                            wqt[:, u * NY + c * P:u * NY + (c + 1) * P], words[:, u, :], ident[:]
+                        )
+            elif phase == 1:
+                wwps = ps_g.tile([P, NY], F32, name="wwps", tag="g")
+                wq_tmp["wwps"] = wwps
+                for c in range(2):
+                    rep = const.tile([P, P], F32, name="rep%d" % c)
+                    nc.vector.tensor_copy(out=rep[:], in_=ww[:, c:c + 1].to_broadcast([P, P]))
+                    nc.tensor.transpose(wwps[:, c * P:(c + 1) * P], rep[:], ident[:])
+                nc.vector.tensor_scalar(
+                    out=wqg[:].rearrange("p (j u e) -> p j u e", u=2, e=2),
+                    in0=wq_tmp["wqt"][:].bitcast(BF16).rearrange("p (u j e) -> p j u e", u=2, e=2),
+                    scalar1=-2.0, scalar2=None, op0=ALU.mult,
                 )
-            wwps = ps_g.tile([P, NY], F32, name="wwps", tag="g")
-            for c in range(2):
-                rep = const.tile([P, P], F32, name="rep%d" % c)
-                nc.vector.tensor_copy(out=rep[:], in_=ww[:, c:c + 1].to_broadcast([P, P]))
-                nc.tensor.transpose(wwps[:, c * P:(c + 1) * P], rep[:], ident[:])
-            nc.vector.tensor_scalar(
-                out=wwb1[:], in0=wwps[:], scalar1=1.0, scalar2=None, op0=ALU.add
-            )
-            wqt = ps_h.tile([P, 512], F32, name="wqt", tag="ht")
-            for c in range(2):
-                words = wq_sb[:, c, :].bitcast(F32).rearrange("j (p u) -> j u p", u=2)
+            else:
+                nc.vector.tensor_scalar(
+                    out=wwb1[:], in0=wq_tmp["wwps"][:], scalar1=1.0, scalar2=None, op0=ALU.add
+                )
+                nc.vector.quantize_mx(
+                    out=wq_codes[:].bitcast(FP8X4), scales=wq_scales[:], in_=wqg[:]
+                )
+
+        def xt_pe(n):
+            i, t = n // T, n % T
+            xt = ps_x.tile([P, 512], F32, name="xt%d" % n, tag="xt")
+            xts[n] = xt
+            words = xs[i][:, t, :].bitcast(F32)
+            for g in range(2):
                 for u in range(2):
                     nc.tensor.transpose(
-                        wqt[:, u * NY + c * P:u * NY + (c + 1) * P], words[:, u, :], ident[:]
+                        xt[:, (u * 2 + g) * P:(u * 2 + g + 1) * P],
+                        words[:, (g * 2 + u) * P:(g * 2 + u + 1) * P],
+                        ident[:],
                     )
-            nc.vector.tensor_scalar(
-                out=wqg[:].rearrange("p (j u e) -> p j u e", u=2, e=2),
-                in0=wqt[:].bitcast(BF16).rearrange("p (u j e) -> p j u e", u=2, e=2),
-                scalar1=-2.0, scalar2=None, op0=ALU.mult,
-            )
-            nc.vector.quantize_mx(
-                out=wq_codes[:].bitcast(FP8X4), scales=wq_scales[:], in_=wqg[:]
-            )
 
-        def stage_xt(i, t):
-            if t == 0:
-                ag[i] = apool.tile([P, 2, BLK, 4], BF16, name="ag%d" % i, tag="ag", align_bytes=64)
-                a_codes[i] = apool.tile([P, 2, BLK], U32, name="ac%d" % i, tag="ac", align_bytes=64)
-                a_scales[i] = apool.tile([P, 2, BLK], U8, name="as%d" % i, tag="as", align_bytes=64)
-            xt = ps_x.tile([P, 512], F32, name="xt%d_%d" % (i, t), tag="xt")
-            words = xs[i][:, t, :].bitcast(F32)
-            for gu in range(4):
-                nc.tensor.transpose(
-                    xt[:, gu * P:(gu + 1) * P], words[:, gu * P:(gu + 1) * P], ident[:]
-                )
-            pairs = xt[:].bitcast(BF16).rearrange("p (g u r e) -> p g r u e", g=2, u=2, e=2)
-            for g in range(2):
-                nc.vector.tensor_scalar(
-                    out=ag[i][:, g, t * P:(t + 1) * P, :].rearrange("p r (u e) -> p r u e", u=2),
-                    in0=pairs[:, g],
-                    scalar1=0.0, scalar2=None, op0=ALU.max,
-                )
-
-        def stage_qa(i, t):
-            for g in range(2):
-                nc.vector.quantize_mx(
-                    out=a_codes[i][:, g, t * P:(t + 1) * P].bitcast(FP8X4),
-                    scales=a_scales[i][:, g, t * P:(t + 1) * P],
-                    in_=ag[i][:, g, t * P:(t + 1) * P, :].rearrange("p r f -> p (r f)"),
-                )
-
-        def stage_l1(i, m):
-            if m == 0:
-                h32[i] = hpool.tile([P, 4, BLK], F32, name="h32_%d" % i, tag="h32")
-            z = ps_z.tile([P, BLK], F32, name="z%d_%d" % (i, m), tag="z")
-            for g in range(2):
+        def l1_pe(n):
+            i, m = n // T, n % T
+            z = ps_z.tile([P, BLK], F32, name="z%d" % n, tag="z")
+            zs[n] = z
+            passes = [(0, True, True)] * DUMMY + [(0, True, False), (1, False, True)]
+            for g, first, last in passes:
                 nc.tensor.matmul_mx(
                     out=z[:],
                     lhsT=wfc_codes[:, g, m * P:(m + 1) * P].bitcast(FP8X4),
                     lhsT_scale=wfc_scales[:, g, m * P:(m + 1) * P],
                     rhs=a_codes[i][:, g, :].bitcast(FP8X4),
                     rhs_scale=a_scales[i][:, g, :],
-                    start=(g == 0), stop=(g == 1),
-                )
-            if s1_on_vector(i, m):
-                nc.vector.tensor_scalar(
-                    out=h32[i][:, m, :], in0=z[:], scalar1=bias[:, m:m + 1], scalar2=0.0,
-                    op0=ALU.add, op1=ALU.max,
-                )
-            else:
-                nc.scalar.activation(
-                    out=h32[i][:, m, :], in_=z[:], func=ACT.Relu, bias=bias[:, m:m + 1], scale=1.0
+                    start=first, stop=last,
                 )
 
-        hg = {}
-
-        def stage_v1(i):
-            hg[i] = gpool.tile([P, BLK, 4], BF16, name="hg%d" % i, tag="hg", align_bytes=64)
-            src = h32[i][:].rearrange("p m b -> p b m")
-            if V1_ON_GPSIMD:
-                nc.gpsimd.tensor_scalar(
-                    out=hg[i][:], in0=src, scalar1=1.0, scalar2=0.0, op0=ALU.mult, op1=ALU.add
-                )
-            else:
-                nc.vector.tensor_copy(out=hg[i][:], in_=src)
-
-        def stage_qh(i):
-            h_codes[i] = hpool.tile([P, BLK], U32, name="hc%d" % i, tag="hc", align_bytes=64)
-            h_scales[i] = hpool.tile([P, BLK], U8, name="hs%d" % i, tag="hs", align_bytes=64)
-            nc.vector.quantize_mx(
-                out=h_codes[i][:].bitcast(FP8X4), scales=h_scales[i][:],
-                in_=hg[i][:].rearrange("p b m -> p (b m)"),
-            )
-
-        def stage_ht(i, t):
-            ht = ps_h.tile([P, 512], F32, name="ht%d_%d" % (i, t), tag="ht")
+        def ht_pe(n):
+            i, t = n // T, n % T
+            ht = ps_h.tile([P, 512], F32, name="ht%d" % n, tag="ht")
+            hts[n] = ht
             for m in range(4):
                 nc.tensor.transpose(
                     ht[:, m * P:(m + 1) * P], h32[i][:, m, t * P:(t + 1) * P], ident[:]
                 )
-            col = i * T + t
-            nc.scalar.activation(
-                out=junk_sq[:], in_=ht[:], func=ACT.Square, accum_out=hh[:, col:col + 1]
-            )
 
-        def stage_l2(i, t):
-            col = i * T + t
-            gp = ps_g.tile([P, NY], F32, name="g%d_%d" % (i, t), tag="g")
+        def l2_pe(n):
+            i, t = n // T, n % T
+            gp = ps_g.tile([P, NY], F32, name="g%d" % n, tag="g")
+            gps[n] = gp
             nc.tensor.matmul_mx(
                 out=gp[:],
                 lhsT=h_codes[i][:, t * P:(t + 1) * P].bitcast(FP8X4),
@@ -228,14 +210,79 @@ def tile_tnet_t_kernel(tc, x, W_fc, b_fc, W_q, out):
                 rhs_scale=wq_scales[:],
                 start=True, stop=True,
             )
+
+        def xe(n):
+            agt[n] = agpool.tile([P, 2, P, 4], BF16, name="ag%d" % n, tag="ag", align_bytes=64)
+            nc.vector.tensor_scalar(
+                out=agt[n][:].rearrange("p g r (u e) -> p (g r) u e", u=2),
+                in0=xts[n][:].bitcast(BF16).rearrange("p (u q e) -> p q u e", u=2, e=2),
+                scalar1=0.0, scalar2=None, op0=ALU.max,
+            )
+
+        def qa(n):
+            i, t = n // T, n % T
+            if t == 0:
+                a_codes[i] = apool.tile([P, 2, BLK], U32, name="ac%d" % i, tag="ac", align_bytes=64)
+                a_scales[i] = apool.tile([P, 2, BLK], U8, name="as%d" % i, tag="as", align_bytes=64)
+            for g in range(2):
+                nc.vector.quantize_mx(
+                    out=a_codes[i][:, g, t * P:(t + 1) * P].bitcast(FP8X4),
+                    scales=a_scales[i][:, g, t * P:(t + 1) * P],
+                    in_=agt[n][:, g, :, :].rearrange("p r f -> p (r f)"),
+                )
+
+        def s1(n):
+            i, m = n // T, n % T
+            if m == 0:
+                h32[i] = hpool.tile([P, 4, BLK], F32, name="h32_%d" % i, tag="h32")
+            if s1_on_vector(i, m):
+                nc.vector.tensor_scalar(
+                    out=h32[i][:, m, :], in0=zs[n][:], scalar1=bias[:, m:m + 1], scalar2=0.0,
+                    op0=ALU.add, op1=ALU.max,
+                )
+            else:
+                nc.scalar.activation(
+                    out=h32[i][:, m, :], in_=zs[n][:], func=ACT.Relu, bias=bias[:, m:m + 1],
+                    scale=1.0,
+                )
+
+        def v1(n):
+            i, c = n // T, n % T
+            hgp[n] = hgpool.tile([P, P, 4], BF16, name="hg%d" % n, tag="hg", align_bytes=64)
+            src = h32[i][:, :, c * P:(c + 1) * P].rearrange("p m b -> p b m")
+            if V1_ON_GPSIMD:
+                nc.gpsimd.tensor_scalar(
+                    out=hgp[n][:], in0=src, scalar1=1.0, scalar2=0.0, op0=ALU.mult, op1=ALU.add
+                )
+            else:
+                nc.vector.tensor_copy(out=hgp[n][:], in_=src)
+
+        def qh(n):
+            i, c = n // T, n % T
+            if c == 0:
+                h_codes[i] = hpool.tile([P, BLK], U32, name="hc%d" % i, tag="hc", align_bytes=64)
+                h_scales[i] = hpool.tile([P, BLK], U8, name="hs%d" % i, tag="hs", align_bytes=64)
+            nc.vector.quantize_mx(
+                out=h_codes[i][:, c * P:(c + 1) * P].bitcast(FP8X4),
+                scales=h_scales[i][:, c * P:(c + 1) * P],
+                in_=hgp[n][:].rearrange("p b m -> p (b m)"),
+            )
+
+        def sq(n):
+            nc.scalar.activation(
+                out=junk_sq[:], in_=hts[n][:], func=ACT.Square, accum_out=hh[:, n:n + 1]
+            )
+
+        def e12(n):
+            i, t = n // T, n % T
             u = u_tiles[i]
             nc.vector.scalar_tensor_tensor(
-                out=u[:, t, :], in0=gp[:], scalar=hh[:, col:col + 1], in1=wwb1[:],
+                out=u[:, t, :], in0=gps[n][:], scalar=hh[:, n:n + 1], in1=wwb1[:],
                 op0=ALU.add, op1=ALU.add,
             )
             nc.vector.tensor_scalar(
                 out=u[:, t, :], in0=u[:, t, :], scalar1=1.0, scalar2=None,
-                op0=ALU.max, op1=ALU.min, accum_out=umin[:, col:col + 1],
+                op0=ALU.max, op1=ALU.min, accum_out=umin[:, n:n + 1],
             )
             if t == T - 1:
                 nc.vector.reciprocal(out=rmin[:, i * T:(i + 1) * T], in_=umin[:, i * T:(i + 1) * T])
@@ -266,7 +313,7 @@ def tile_tnet_t_kernel(tc, x, W_fc, b_fc, W_q, out):
                     nc.scalar.activation(out=lns[:, c0:c1], in_=ssum[:, c0:c1], func=ACT.Ln)
                     for i in GROUPS[a]:
                         for tt in range(T):
-                            fins.append((a, i, tt))
+                            fins.append((i, tt))
                 else:
                     col = a * T + t
                     u = u_tiles[a]
@@ -282,14 +329,13 @@ def tile_tnet_t_kernel(tc, x, W_fc, b_fc, W_q, out):
                 state["unit"] += 1
                 n += 1
 
-        def emit_fins(limit):
+        def emit_fins(limit, upto):
             n = 0
-            while state["fin"] < len(fins) and n < limit:
-                q, i, t = fins[state["fin"]]
+            while state["fin"] < min(upto, len(fins)) and n < limit:
+                i, t = fins[state["fin"]]
                 col = i * T + t
                 u = u_tiles[i]
-                eng = nc.vector if q in FIN_V_GROUPS else nc.gpsimd
-                eng.tensor_scalar(
+                nc.vector.tensor_scalar(
                     out=u[:, t, :], in0=u[:, t, :], scalar1=lns[:, col:col + 1], scalar2=-1.0,
                     op0=ALU.add, op1=ALU.mult,
                 )
@@ -301,6 +347,9 @@ def tile_tnet_t_kernel(tc, x, W_fc, b_fc, W_q, out):
                 state["fin"] += 1
                 n += 1
 
+        def ok(n):
+            return 0 <= n < NT
+
         nc.sync.dma_start(out=wfc_sb[:], in_=W_fc.rearrange("(p m) k -> p m k", m=4))
         nc.scalar.dma_start(out=b_bf[:], in_=b_fc.rearrange("(p m) -> p m", m=4))
         nc.scalar.dma_start(out=wq_sb[:], in_=W_q.rearrange("(c j) k -> j c k", c=2))
@@ -309,32 +358,42 @@ def tile_tnet_t_kernel(tc, x, W_fc, b_fc, W_q, out):
         make_identity(nc, ident[:])
         setup_wfc()
 
-        for k in range(-1, NB + 2):
-            for t in range(T):
-                if t == 0:
-                    if 0 <= k < NB:
-                        stage_qa(k, T - 1)
-                elif 0 <= k + 1 < NB:
-                    stage_qa(k + 1, t - 1)
-                if 0 <= k + 1 < NB:
-                    stage_xt(k + 1, t)
-                if 0 <= k - 1 < NB:
-                    if t == 0:
-                        stage_v1(k - 1)
-                    stage_ht(k - 1, t)
-                if 0 <= k < NB:
-                    stage_l1(k, t)
-                if 0 <= k - 2 < NB:
-                    stage_l2(k - 2, t)
-                    if t == T - 1:
-                        state["ready"] = k - 2
-                if t == 2 and 0 <= k - 1 < NB:
-                    stage_qh(k - 1)
-                emit_units(SLICES_PER_QUARTER)
-                emit_fins(FIN_PER_QUARTER)
-            if k == -1:
-                setup_wq()
-            if 0 <= k + 1 + X_BUFS < NB + 0 and k + 1 >= 0:
-                load(k + 1 + X_BUFS - 0)
+        fin_hist = []
+        for step in range(NT + LAG_E + 1):
+            if ok(step):
+                xt_pe(step)
+            if ok(step - LAG_HT):
+                ht_pe(step - LAG_HT)
+            if ok(step - LAG_L1):
+                l1_pe(step - LAG_L1)
+            if ok(step - LAG_L2):
+                l2_pe(step - LAG_L2)
+
+            if ok(step - LAG_QA):
+                qa(step - LAG_QA)
+            if ok(step - LAG_XE):
+                xe(step - LAG_XE)
+            if ok(step - LAG_SQ):
+                sq(step - LAG_SQ)
+            if ok(step - LAG_S1):
+                s1(step - LAG_S1)
+            if ok(step - LAG_V1):
+                v1(step - LAG_V1)
+            if ok(step - LAG_QH):
+                qh(step - LAG_QH)
+            if ok(step - LAG_E):
+                e12(step - LAG_E)
+            if step >= FIN_LAG:
+                emit_fins(FINS_PER_STEP, fin_hist[step - FIN_LAG])
+            done = step - LAG_E - LN_LAG
+            if done >= T - 1:
+                state["ready"] = min(NB - 1, (done + 1) // T - 1)
+            emit_units(UNITS_PER_STEP)
+            fin_hist.append(len(fins))
+            if WQ_AT <= step < WQ_AT + 3:
+                setup_wq(step - WQ_AT)
+            if step % T == T - 1 and step // T + X_BUFS < NB:
+                load(step // T + X_BUFS)
+        state["ready"] = NB - 1
         emit_units(len(units))
-        emit_fins(len(fins))
+        emit_fins(len(fins), len(fins))

@@ -273,13 +273,17 @@ def tile_tnet_t_kernel(tc, x, W_fc, b_fc, W_q, out):
                 out=junk_sq[:], in_=hts[n][:], func=ACT.Square, accum_out=hh[:, n:n + 1]
             )
 
-        def e12(n):
+        def e1(n):
             i, t = n // T, n % T
             u = u_tiles[i]
             nc.vector.scalar_tensor_tensor(
                 out=u[:, t, :], in0=gps[n][:], scalar=hh[:, n:n + 1], in1=wwb1[:],
                 op0=ALU.add, op1=ALU.add,
             )
+
+        def e2(n):
+            i, t = n // T, n % T
+            u = u_tiles[i]
             nc.vector.tensor_scalar(
                 out=u[:, t, :], in0=u[:, t, :], scalar1=1.0, scalar2=None,
                 op0=ALU.max, op1=ALU.min, accum_out=umin[:, n:n + 1],
@@ -369,20 +373,22 @@ def tile_tnet_t_kernel(tc, x, W_fc, b_fc, W_q, out):
             if ok(step - LAG_L2):
                 l2_pe(step - LAG_L2)
 
-            if ok(step - LAG_QA):
-                qa(step - LAG_QA)
             if ok(step - LAG_XE):
                 xe(step - LAG_XE)
+            if ok(step - LAG_E):
+                e1(step - LAG_E)
             if ok(step - LAG_SQ):
                 sq(step - LAG_SQ)
             if ok(step - LAG_S1):
                 s1(step - LAG_S1)
+            if ok(step - LAG_QA):
+                qa(step - LAG_QA)
             if ok(step - LAG_V1):
                 v1(step - LAG_V1)
             if ok(step - LAG_QH):
                 qh(step - LAG_QH)
             if ok(step - LAG_E):
-                e12(step - LAG_E)
+                e2(step - LAG_E)
             if step >= FIN_LAG:
                 emit_fins(FINS_PER_STEP, fin_hist[step - FIN_LAG])
             done = step - LAG_E - LN_LAG

@@ -19,14 +19,13 @@ T = BLK // P
 NT = NB * T
 FLOPS = 2 * B * NX * NH + 2 * B * NH * NY
 
-GROUPS = [[0,1,2,3],[4,5,6,7],[8,9,10,11],[12,13,14],[15]]
+GROUPS = [[0,1,2,3,4,5],[6,7,8,9,10],[11,12,13],[14,15]]
 UNITS_PER_STEP = 3
 FINS_PER_STEP = 2
 FIN_LAG = 2
 LN_LAG = 1
-DUMMY = 1
-V1_ON_GPSIMD = False
-HG_BUFS = 3
+V1_ON_GPSIMD = True
+HG_BUFS = 1
 X_BUFS = 4
 WQ_AT = 3
 LAG_XE = 1
@@ -39,10 +38,15 @@ LAG_SQ = 12
 LAG_QH = 12
 LAG_L2 = 13
 LAG_E = 14
+LAG_E2 = 15
+
+
+def dummies(n):
+    return 1 - n % 2
 
 
 def s1_on_vector(i, m):
-    return i >= 13 and m % 2 == 1
+    return m == 1 or (i >= 13 and m == 3)
 
 
 def tile_tnet_t_kernel(tc, x, W_fc, b_fc, W_q, out):
@@ -178,7 +182,7 @@ def tile_tnet_t_kernel(tc, x, W_fc, b_fc, W_q, out):
             i, m = n // T, n % T
             z = ps_z.tile([P, BLK], F32, name="z%d" % n, tag="z")
             zs[n] = z
-            passes = [(0, True, True)] * DUMMY + [(0, True, False), (1, False, True)]
+            passes = [(0, True, True)] * dummies(n) + [(0, True, False), (1, False, True)]
             for g, first, last in passes:
                 nc.tensor.matmul_mx(
                     out=z[:],
@@ -363,7 +367,7 @@ def tile_tnet_t_kernel(tc, x, W_fc, b_fc, W_q, out):
         setup_wfc()
 
         fin_hist = []
-        for step in range(NT + LAG_E + 1):
+        for step in range(NT + LAG_E2 + 1):
             if ok(step):
                 xt_pe(step)
             if ok(step - LAG_HT):
@@ -373,6 +377,14 @@ def tile_tnet_t_kernel(tc, x, W_fc, b_fc, W_q, out):
             if ok(step - LAG_L2):
                 l2_pe(step - LAG_L2)
 
+            if ok(step - LAG_QA):
+                qa(step - LAG_QA)
+            if step >= FIN_LAG:
+                emit_fins(FINS_PER_STEP, fin_hist[step - FIN_LAG])
+            if ok(step - LAG_QH):
+                qh(step - LAG_QH)
+            if ok(step - LAG_V1):
+                v1(step - LAG_V1)
             if ok(step - LAG_XE):
                 xe(step - LAG_XE)
             if ok(step - LAG_E):
@@ -381,17 +393,9 @@ def tile_tnet_t_kernel(tc, x, W_fc, b_fc, W_q, out):
                 sq(step - LAG_SQ)
             if ok(step - LAG_S1):
                 s1(step - LAG_S1)
-            if ok(step - LAG_QA):
-                qa(step - LAG_QA)
-            if ok(step - LAG_V1):
-                v1(step - LAG_V1)
-            if ok(step - LAG_QH):
-                qh(step - LAG_QH)
-            if ok(step - LAG_E):
-                e2(step - LAG_E)
-            if step >= FIN_LAG:
-                emit_fins(FINS_PER_STEP, fin_hist[step - FIN_LAG])
-            done = step - LAG_E - LN_LAG
+            if ok(step - LAG_E2):
+                e2(step - LAG_E2)
+            done = step - LAG_E2 - LN_LAG
             if done >= T - 1:
                 state["ready"] = min(NB - 1, (done + 1) // T - 1)
             emit_units(UNITS_PER_STEP)

@@ -27,7 +27,7 @@ LN_LAG = 1
 V1_ON_GPSIMD = True
 HG_BUFS = 1
 X_BUFS = 4
-WQ_AT = 3
+WQ_AT = 7
 LAG_XE = 1
 LAG_QA = 2
 LAG_L1 = 6
@@ -46,7 +46,7 @@ def dummies(n):
 
 
 def s1_on_vector(i, m):
-    return m == 1 or (i >= 13 and m == 3)
+    return (i >= 8 and m == 1) or (i >= 12 and m == 3)
 
 
 def tile_tnet_t_kernel(tc, x, W_fc, b_fc, W_q, out):
@@ -100,35 +100,44 @@ def tile_tnet_t_kernel(tc, x, W_fc, b_fc, W_q, out):
         gps = {}
         wq_tmp = {}
 
-        def load(i):
-            xs[i] = xpool.tile([P, T, NX], BF16, name="x%d" % i, tag="x")
+        def load(i, pieces):
+            if pieces[0] == 0:
+                xs[i] = xpool.tile([P, T, NX], BF16, name="x%d" % i, tag="x")
+            src = x[i * BLK:(i + 1) * BLK, :].rearrange("(p t) k -> p t k", t=T)
+            t0, t1 = pieces
+            nc.sync.dma_start(out=xs[i][:, t0:t1, :], in_=src[:, t0:t1, :])
+
+        def load_wfc(m):
             nc.sync.dma_start(
-                out=xs[i][:],
-                in_=x[i * BLK:(i + 1) * BLK, :].rearrange("(p t) k -> p t k", t=T),
+                out=wfc_sb[:, m, :], in_=W_fc.rearrange("(p m) k -> p m k", m=4)[:, m, :]
             )
 
-        def setup_wfc():
-            for m in range(4):
-                wt = ps_x.tile([P, 512], F32, name="wt%d" % m, tag="xt")
-                words = wfc_sb[:, m, :].bitcast(F32)
-                for gu in range(4):
-                    nc.tensor.transpose(
-                        wt[:, gu * P:(gu + 1) * P], words[:, gu * P:(gu + 1) * P], ident[:]
-                    )
-                dst = wg[:].bitcast(F32).rearrange("p (g c u) -> p g c u", g=2, u=2)
-                dst = dst[:, :, m * P:(m + 1) * P, :]
-                src = wt[:].rearrange("p (g u n) -> p g n u", g=2, u=2)
-                if m % 2 == 0:
-                    nc.vector.tensor_copy(out=dst, in_=src)
-                else:
-                    nc.scalar.copy(out=dst, in_=src)
-            for g in range(2):
-                nc.vector.quantize_mx(
-                    out=wfc_codes[:, g, :].bitcast(FP8X4),
-                    scales=wfc_scales[:, g, :],
-                    in_=wg[:, g * NH * 4:(g + 1) * NH * 4],
+        wts = {}
+
+        def wfc_pe(m):
+            wt = ps_h.tile([P, 512], F32, name="wt%d" % m, tag="ht")
+            wts[m] = wt
+            words = wfc_sb[:, m, :].bitcast(F32)
+            for gu in range(4):
+                nc.tensor.transpose(
+                    wt[:, gu * P:(gu + 1) * P], words[:, gu * P:(gu + 1) * P], ident[:]
                 )
-            nc.vector.tensor_copy(out=bias[:], in_=b_bf[:])
+
+        def wfc_exit(m):
+            dst = wg[:].bitcast(F32).rearrange("p (g c u) -> p g c u", g=2, u=2)
+            nc.scalar.copy(
+                out=dst[:, :, m * P:(m + 1) * P, :],
+                in_=wts[m][:].rearrange("p (g u n) -> p g n u", g=2, u=2),
+            )
+
+        def wfc_quant(m):
+            for g in range(2):
+                c0 = g * NH + m * P
+                nc.vector.quantize_mx(
+                    out=wfc_codes[:, g, m * P:(m + 1) * P].bitcast(FP8X4),
+                    scales=wfc_scales[:, g, m * P:(m + 1) * P],
+                    in_=wg[:, c0 * 4:(c0 + P) * 4],
+                )
 
         def setup_wq(phase):
             if phase == 0:
@@ -358,18 +367,34 @@ def tile_tnet_t_kernel(tc, x, W_fc, b_fc, W_q, out):
         def ok(n):
             return 0 <= n < NT
 
-        nc.sync.dma_start(out=wfc_sb[:], in_=W_fc.rearrange("(p m) k -> p m k", m=4))
+        make_identity(nc, ident[:])
+        load(0, (0, 1))
+        load(0, (1, 2))
+        load_wfc(0)
+        load(0, (2, 3))
+        load_wfc(1)
+        load(0, (3, 4))
+        load_wfc(2)
+        load_wfc(3)
+        load(1, (0, 2))
+        load(1, (2, 4))
         nc.scalar.dma_start(out=b_bf[:], in_=b_fc.rearrange("(p m) -> p m", m=4))
         nc.scalar.dma_start(out=wq_sb[:], in_=W_q.rearrange("(c j) k -> j c k", c=2))
-        for i in range(X_BUFS):
-            load(i)
-        make_identity(nc, ident[:])
-        setup_wfc()
+        for i in range(2, X_BUFS):
+            load(i, (0, T))
 
         fin_hist = []
         for step in range(NT + LAG_E2 + 1):
             if ok(step):
                 xt_pe(step)
+            if 0 <= step - 1 < 4:
+                wfc_pe(step - 1)
+            if 0 <= step - 2 < 4:
+                wfc_exit(step - 2)
+            if 0 <= step - 3 < 4:
+                wfc_quant(step - 3)
+            if step == 4:
+                nc.vector.tensor_copy(out=bias[:], in_=b_bf[:])
             if ok(step - LAG_HT):
                 ht_pe(step - LAG_HT)
             if ok(step - LAG_L1):
@@ -403,7 +428,7 @@ def tile_tnet_t_kernel(tc, x, W_fc, b_fc, W_q, out):
             if WQ_AT <= step < WQ_AT + 3:
                 setup_wq(step - WQ_AT)
             if step % T == T - 1 and step // T + X_BUFS < NB:
-                load(step // T + X_BUFS)
+                load(step // T + X_BUFS, (0, T))
         state["ready"] = NB - 1
         emit_units(len(units))
         emit_fins(len(fins), len(fins))

@@ -21,7 +21,8 @@ FLOPS = 2 * B * NX * NH + 2 * B * NH * NY
 
 GROUPS = [[0,1,2,3,4,5],[6,7,8,9,10],[11,12,13],[14,15]]
 UNITS_PER_STEP = 3
-FINS_PER_STEP = 2
+FINS_V = 1
+FINS_G = 1
 FIN_LAG = 2
 LN_LAG = 1
 V1_ON_GPSIMD = True
@@ -45,8 +46,12 @@ def dummies(n):
     return 1 - n % 2
 
 
+def xe_on_scalar(n):
+    return False
+
+
 def s1_on_vector(i, m):
-    return (i >= 8 and m == 1) or (i >= 12 and m == 3)
+    return (i >= 6 and m == 1) or (i >= 10 and m == 3) or (i >= 13 and m == 0)
 
 
 def tile_tnet_t_kernel(tc, x, W_fc, b_fc, W_q, out):
@@ -81,7 +86,8 @@ def tile_tnet_t_kernel(tc, x, W_fc, b_fc, W_q, out):
         junk_ex = const.tile([P, NY], BF16, name="junk_ex")
         hh = const.tile([P, NT], F32, name="hh")
         umin = const.tile([P, NT], F32, name="umin")
-        rmin = const.tile([P, NT], F32, name="rmin")
+        lmin = const.tile([P, NT], F32, name="lmin")
+        shift = const.tile([P, NT], F32, name="shift")
         ssum = const.tile([P, NT], F32, name="ssum")
         lns = const.tile([P, NT], F32, name="lns")
         u_tiles = [const.tile([P, T, NY], F32, name="u%d" % i) for i in range(NB)]
@@ -226,11 +232,12 @@ def tile_tnet_t_kernel(tc, x, W_fc, b_fc, W_q, out):
 
         def xe(n):
             agt[n] = agpool.tile([P, 2, P, 4], BF16, name="ag%d" % n, tag="ag", align_bytes=64)
-            nc.vector.tensor_scalar(
-                out=agt[n][:].rearrange("p g r (u e) -> p (g r) u e", u=2),
-                in0=xts[n][:].bitcast(BF16).rearrange("p (u q e) -> p q u e", u=2, e=2),
-                scalar1=0.0, scalar2=None, op0=ALU.max,
-            )
+            dst = agt[n][:].rearrange("p g r (u e) -> p (g r) u e", u=2)
+            src = xts[n][:].bitcast(BF16).rearrange("p (u q e) -> p q u e", u=2, e=2)
+            if xe_on_scalar(n):
+                nc.scalar.activation(out=dst, in_=src, func=ACT.Relu)
+            else:
+                nc.vector.tensor_scalar(out=dst, in0=src, scalar1=0.0, scalar2=None, op0=ALU.max)
 
         def qa(n):
             i, t = n // T, n % T
@@ -301,8 +308,6 @@ def tile_tnet_t_kernel(tc, x, W_fc, b_fc, W_q, out):
                 out=u[:, t, :], in0=u[:, t, :], scalar1=1.0, scalar2=None,
                 op0=ALU.max, op1=ALU.min, accum_out=umin[:, n:n + 1],
             )
-            if t == T - 1:
-                nc.vector.reciprocal(out=rmin[:, i * T:(i + 1) * T], in_=umin[:, i * T:(i + 1) * T])
 
         units = []
         for q in range(len(GROUPS)):
@@ -311,6 +316,7 @@ def tile_tnet_t_kernel(tc, x, W_fc, b_fc, W_q, out):
             for i in GROUPS[q]:
                 for t in range(T):
                     units.append(("LN", i, t))
+            units.append(("LM", q, 0))
             for i in GROUPS[q]:
                 for t in range(T):
                     units.append(("EX", i, t))
@@ -322,12 +328,17 @@ def tile_tnet_t_kernel(tc, x, W_fc, b_fc, W_q, out):
             n = 0
             while state["unit"] < len(units) and n < limit:
                 kind, a, t = units[state["unit"]]
-                if kind != "LS" and a > state["ready"]:
+                if kind == "LN" and a * T + t > state["ready"]:
                     return
-                if kind == "LS":
+                if kind == "LM":
+                    c0 = GROUPS[a][0] * T
+                    c1 = (GROUPS[a][-1] + 1) * T
+                    nc.scalar.activation(out=lmin[:, c0:c1], in_=umin[:, c0:c1], func=ACT.Ln)
+                elif kind == "LS":
                     c0 = GROUPS[a][0] * T
                     c1 = (GROUPS[a][-1] + 1) * T
                     nc.scalar.activation(out=lns[:, c0:c1], in_=ssum[:, c0:c1], func=ACT.Ln)
+                    fins.append((a, -1))
                     for i in GROUPS[a]:
                         for tt in range(T):
                             fins.append((i, tt))
@@ -335,27 +346,34 @@ def tile_tnet_t_kernel(tc, x, W_fc, b_fc, W_q, out):
                     col = a * T + t
                     u = u_tiles[a]
                     if kind == "LN":
-                        nc.scalar.activation(
-                            out=u[:, t, :], in_=u[:, t, :], func=ACT.Ln, scale=rmin[:, col:col + 1]
-                        )
+                        nc.scalar.activation(out=u[:, t, :], in_=u[:, t, :], func=ACT.Ln)
                     else:
                         nc.scalar.activation(
                             out=junk_ex[:], in_=u[:, t, :], func=ACT.Exp, scale=-1.0,
-                            accum_out=ssum[:, col:col + 1],
+                            bias=lmin[:, col:col + 1], accum_out=ssum[:, col:col + 1],
                         )
                 state["unit"] += 1
                 n += 1
 
-        def emit_fins(limit, upto):
+        def emit_fins(limit, upto, eng):
             n = 0
             while state["fin"] < min(upto, len(fins)) and n < limit:
                 i, t = fins[state["fin"]]
-                col = i * T + t
-                u = u_tiles[i]
-                nc.vector.tensor_scalar(
-                    out=u[:, t, :], in0=u[:, t, :], scalar1=lns[:, col:col + 1], scalar2=-1.0,
-                    op0=ALU.add, op1=ALU.mult,
-                )
+                if t < 0 and eng is not nc.vector:
+                    return
+                if t < 0:
+                    c0 = GROUPS[i][0] * T
+                    c1 = (GROUPS[i][-1] + 1) * T
+                    nc.vector.tensor_tensor(
+                        out=shift[:, c0:c1], in0=lmin[:, c0:c1], in1=lns[:, c0:c1], op=ALU.subtract
+                    )
+                else:
+                    col = i * T + t
+                    u = u_tiles[i]
+                    eng.tensor_scalar(
+                        out=u[:, t, :], in0=u[:, t, :], scalar1=-1.0,
+                        scalar2=shift[:, col:col + 1], op0=ALU.mult, op1=ALU.add,
+                    )
                 if t == T - 1:
                     nc.sync.dma_start(
                         out=out[i * BLK:(i + 1) * BLK, :].rearrange("(p t) j -> p t j", t=T),
@@ -405,11 +423,13 @@ def tile_tnet_t_kernel(tc, x, W_fc, b_fc, W_q, out):
             if ok(step - LAG_QA):
                 qa(step - LAG_QA)
             if step >= FIN_LAG:
-                emit_fins(FINS_PER_STEP, fin_hist[step - FIN_LAG])
+                emit_fins(FINS_V, fin_hist[step - FIN_LAG], nc.vector)
             if ok(step - LAG_QH):
                 qh(step - LAG_QH)
             if ok(step - LAG_V1):
                 v1(step - LAG_V1)
+            if step >= FIN_LAG:
+                emit_fins(FINS_G, fin_hist[step - FIN_LAG], nc.gpsimd)
             if ok(step - LAG_XE):
                 xe(step - LAG_XE)
             if ok(step - LAG_E):
@@ -421,14 +441,13 @@ def tile_tnet_t_kernel(tc, x, W_fc, b_fc, W_q, out):
             if ok(step - LAG_E2):
                 e2(step - LAG_E2)
             done = step - LAG_E2 - LN_LAG
-            if done >= T - 1:
-                state["ready"] = min(NB - 1, (done + 1) // T - 1)
+            state["ready"] = min(NT - 1, done)
             emit_units(UNITS_PER_STEP)
             fin_hist.append(len(fins))
             if WQ_AT <= step < WQ_AT + 3:
                 setup_wq(step - WQ_AT)
             if step % T == T - 1 and step // T + X_BUFS < NB:
                 load(step // T + X_BUFS, (0, T))
-        state["ready"] = NB - 1
+        state["ready"] = NT - 1
         emit_units(len(units))
-        emit_fins(len(fins), len(fins))
+        emit_fins(len(fins), len(fins), nc.vector)

@@ -20,7 +20,10 @@ NT = NB * T
 FLOPS = 2 * B * NX * NH + 2 * B * NH * NY
 
 GROUPS = [[0,1,2,3,4,5],[6,7,8,9,10],[11,12,13],[14,15]]
-UNITS_PER_STEP = 3
+UNITS_PER_STEP = 2
+UNITS_FREE = 4
+UNITS_SWITCH = 1
+SWITCH_S1V = True
 FINS_V = 1
 FINS_G = 1
 FIN_LAG = 2
@@ -255,7 +258,8 @@ def tile_tnet_t_kernel(tc, x, W_fc, b_fc, W_q, out):
             i, m = n // T, n % T
             if m == 0:
                 h32[i] = hpool.tile([P, 4, BLK], F32, name="h32_%d" % i, tag="h32")
-            if s1_on_vector(i, m):
+            state["s1v"] = s1_on_vector(i, m) or (SWITCH_S1V and next_unit_switches())
+            if state["s1v"]:
                 nc.vector.tensor_scalar(
                     out=h32[i][:, m, :], in0=zs[n][:], scalar1=bias[:, m:m + 1], scalar2=0.0,
                     op0=ALU.add, op1=ALU.max,
@@ -321,7 +325,15 @@ def tile_tnet_t_kernel(tc, x, W_fc, b_fc, W_q, out):
                 for t in range(T):
                     units.append(("EX", i, t))
         units.append(("LS", len(GROUPS) - 1, 0))
-        state = {"unit": 0, "ready": -1, "fin": 0}
+        state = {"unit": 0, "ready": -1, "fin": 0, "table": "", "s1v": False}
+
+        def next_unit_switches():
+            if state["unit"] >= len(units):
+                return False
+            kind, a, t = units[state["unit"]]
+            if kind == "LN" and a * T + t > state["ready"]:
+                return False
+            return ("EX" if kind == "EX" else "LN") != state["table"]
         fins = []
 
         def emit_units(limit):
@@ -352,6 +364,7 @@ def tile_tnet_t_kernel(tc, x, W_fc, b_fc, W_q, out):
                             out=junk_ex[:], in_=u[:, t, :], func=ACT.Exp, scale=-1.0,
                             bias=lmin[:, col:col + 1], accum_out=ssum[:, col:col + 1],
                         )
+                state["table"] = "EX" if kind == "EX" else "LN"
                 state["unit"] += 1
                 n += 1
 
@@ -442,7 +455,13 @@ def tile_tnet_t_kernel(tc, x, W_fc, b_fc, W_q, out):
                 e2(step - LAG_E2)
             done = step - LAG_E2 - LN_LAG
             state["ready"] = min(NT - 1, done)
-            emit_units(UNITS_PER_STEP)
+            if next_unit_switches():
+                emit_units(UNITS_SWITCH)
+            elif state["s1v"] or not ok(step - LAG_S1):
+                emit_units(UNITS_FREE)
+            else:
+                emit_units(UNITS_PER_STEP)
+            state["s1v"] = False
             fin_hist.append(len(fins))
             if WQ_AT <= step < WQ_AT + 3:
                 setup_wq(step - WQ_AT)

@@ -20,7 +20,7 @@ NT = NB * T
 FLOPS = 2 * B * NX * NH + 2 * B * NH * NY
 
 GROUPS = [[0,1,2,3,4,5],[6,7,8,9,10],[11,12,13],[14,15]]
-UNITS_PER_STEP = 2
+UNITS_PER_STEP = 1
 UNITS_FREE = 4
 UNITS_SWITCH = 1
 SWITCH_S1V = True
@@ -28,6 +28,7 @@ FINS_V = 1
 FINS_G = 1
 FIN_LAG = 2
 LN_LAG = 1
+LNW = 4
 V1_ON_GPSIMD = True
 HG_BUFS = 1
 X_BUFS = 4
@@ -318,7 +319,7 @@ def tile_tnet_t_kernel(tc, x, W_fc, b_fc, W_q, out):
             if q > 0:
                 units.append(("LS", q - 1, 0))
             for i in GROUPS[q]:
-                for t in range(T):
+                for t in range(0, T, LNW):
                     units.append(("LN", i, t))
             units.append(("LM", q, 0))
             for i in GROUPS[q]:
@@ -331,7 +332,7 @@ def tile_tnet_t_kernel(tc, x, W_fc, b_fc, W_q, out):
             if state["unit"] >= len(units):
                 return False
             kind, a, t = units[state["unit"]]
-            if kind == "LN" and a * T + t > state["ready"]:
+            if kind == "LN" and a * T + t + LNW - 1 > state["ready"]:
                 return False
             return ("EX" if kind == "EX" else "LN") != state["table"]
         fins = []
@@ -340,7 +341,7 @@ def tile_tnet_t_kernel(tc, x, W_fc, b_fc, W_q, out):
             n = 0
             while state["unit"] < len(units) and n < limit:
                 kind, a, t = units[state["unit"]]
-                if kind == "LN" and a * T + t > state["ready"]:
+                if kind == "LN" and a * T + t + LNW - 1 > state["ready"]:
                     return
                 if kind == "LM":
                     c0 = GROUPS[a][0] * T
@@ -358,7 +359,10 @@ def tile_tnet_t_kernel(tc, x, W_fc, b_fc, W_q, out):
                     col = a * T + t
                     u = u_tiles[a]
                     if kind == "LN":
-                        nc.scalar.activation(out=u[:, t, :], in_=u[:, t, :], func=ACT.Ln)
+                        nc.scalar.activation(
+                            out=u[:, t:t + LNW, :], in_=u[:, t:t + LNW, :], func=ACT.Ln
+                        )
+                        n += LNW - 1
                     else:
                         nc.scalar.activation(
                             out=junk_ex[:], in_=u[:, t, :], func=ACT.Exp, scale=-1.0,

@@ -47,7 +47,7 @@ LAG_E2 = 15
 
 
 def dummies(n):
-    return 1 - n % 2
+    return 0
 
 
 def xe_on_scalar(n):

@@ -24,26 +24,26 @@ UNITS_PER_STEP = 1
 UNITS_FREE = 4
 UNITS_SWITCH = 1
 SWITCH_S1V = True
-FINS_V = 1
-FINS_G = 1
 FIN_LAG = 2
 LN_LAG = 1
 LNW = 4
-V1_ON_GPSIMD = True
+V1G = lambda i, c: True
+FG = lambda s: 0 if 64 <= s < 74 else 1
+FV = lambda s: 1
 HG_BUFS = 1
 X_BUFS = 4
-WQ_AT = 7
+WQ_AT = 6
 LAG_XE = 1
-LAG_QA = 2
-LAG_L1 = 6
-LAG_S1 = 7
-LAG_V1 = 11
-LAG_HT = 11
-LAG_SQ = 12
-LAG_QH = 12
-LAG_L2 = 13
-LAG_E = 14
-LAG_E2 = 15
+LAG_QA = 3
+LAG_L1 = 7
+LAG_S1 = 8
+LAG_V1 = 12
+LAG_HT = 12
+LAG_SQ = 13
+LAG_QH = 13
+LAG_L2 = 14
+LAG_E = 15
+LAG_E2 = 16
 
 
 def dummies(n):
@@ -55,7 +55,7 @@ def xe_on_scalar(n):
 
 
 def s1_on_vector(i, m):
-    return (i >= 6 and m == 1) or (i >= 10 and m == 3) or (i >= 13 and m == 0)
+    return (i >= 8 and m == 1) or i >= 14
 
 
 def tile_tnet_t_kernel(tc, x, W_fc, b_fc, W_q, out):
@@ -63,7 +63,7 @@ def tile_tnet_t_kernel(tc, x, W_fc, b_fc, W_q, out):
     with ExitStack() as ctx:
         const = ctx.enter_context(tc.tile_pool(name="const", bufs=1))
         xpool = ctx.enter_context(tc.tile_pool(name="xpool", bufs=X_BUFS))
-        agpool = ctx.enter_context(tc.tile_pool(name="agpool", bufs=3))
+        agpool = ctx.enter_context(tc.tile_pool(name="agpool", bufs=2))
         apool = ctx.enter_context(tc.tile_pool(name="apool", bufs=2))
         hpool = ctx.enter_context(tc.tile_pool(name="hpool", bufs=3))
         hgpool = ctx.enter_context(tc.tile_pool(name="hgpool", bufs=HG_BUFS))
@@ -235,25 +235,29 @@ def tile_tnet_t_kernel(tc, x, W_fc, b_fc, W_q, out):
             )
 
         def xe(n):
-            agt[n] = agpool.tile([P, 2, P, 4], BF16, name="ag%d" % n, tag="ag", align_bytes=64)
-            dst = agt[n][:].rearrange("p g r (u e) -> p (g r) u e", u=2)
-            src = xts[n][:].bitcast(BF16).rearrange("p (u q e) -> p q u e", u=2, e=2)
+            if n % 2 == 0:
+                agt[n // 2] = agpool.tile(
+                    [P, 2, 2, P, 4], BF16, name="ag%d" % n, tag="ag", align_bytes=64
+                )
+            dst = agt[n // 2][:, :, n % 2, :, :].rearrange("p g r (u e) -> p g r u e", u=2)
+            src = xts[n][:].bitcast(BF16).rearrange("p (u g r e) -> p g r u e", u=2, g=2, e=2)
             if xe_on_scalar(n):
                 nc.scalar.activation(out=dst, in_=src, func=ACT.Relu)
             else:
                 nc.vector.tensor_scalar(out=dst, in0=src, scalar1=0.0, scalar2=None, op0=ALU.max)
 
         def qa(n):
+            pair, g = n // 2, n % 2
             i, t = n // T, n % T
             if t == 0:
                 a_codes[i] = apool.tile([P, 2, BLK], U32, name="ac%d" % i, tag="ac", align_bytes=64)
                 a_scales[i] = apool.tile([P, 2, BLK], U8, name="as%d" % i, tag="as", align_bytes=64)
-            for g in range(2):
-                nc.vector.quantize_mx(
-                    out=a_codes[i][:, g, t * P:(t + 1) * P].bitcast(FP8X4),
-                    scales=a_scales[i][:, g, t * P:(t + 1) * P],
-                    in_=agt[n][:, g, :, :].rearrange("p r f -> p (r f)"),
-                )
+            c0 = (pair % 2) * 2 * P
+            nc.vector.quantize_mx(
+                out=a_codes[i][:, g, c0:c0 + 2 * P].bitcast(FP8X4),
+                scales=a_scales[i][:, g, c0:c0 + 2 * P],
+                in_=agt[pair][:, g, :, :, :].rearrange("p t r f -> p (t r f)"),
+            )
 
         def s1(n):
             i, m = n // T, n % T
@@ -275,7 +279,7 @@ def tile_tnet_t_kernel(tc, x, W_fc, b_fc, W_q, out):
             i, c = n // T, n % T
             hgp[n] = hgpool.tile([P, P, 4], BF16, name="hg%d" % n, tag="hg", align_bytes=64)
             src = h32[i][:, :, c * P:(c + 1) * P].rearrange("p m b -> p b m")
-            if V1_ON_GPSIMD:
+            if V1G(i, c):
                 nc.gpsimd.tensor_scalar(
                     out=hgp[n][:], in0=src, scalar1=1.0, scalar2=0.0, op0=ALU.mult, op1=ALU.add
                 )
@@ -440,13 +444,13 @@ def tile_tnet_t_kernel(tc, x, W_fc, b_fc, W_q, out):
             if ok(step - LAG_QA):
                 qa(step - LAG_QA)
             if step >= FIN_LAG:
-                emit_fins(FINS_V, fin_hist[step - FIN_LAG], nc.vector)
+                emit_fins(FV(step), fin_hist[step - FIN_LAG], nc.vector)
             if ok(step - LAG_QH):
                 qh(step - LAG_QH)
             if ok(step - LAG_V1):
                 v1(step - LAG_V1)
             if step >= FIN_LAG:
-                emit_fins(FINS_G, fin_hist[step - FIN_LAG], nc.gpsimd)
+                emit_fins(FG(step), fin_hist[step - FIN_LAG], nc.gpsimd)
             if ok(step - LAG_XE):
                 xe(step - LAG_XE)
             if ok(step - LAG_E):

@@ -22,13 +22,13 @@ FLOPS = 2 * B * NX * NH + 2 * B * NH * NY
 GROUPS = [[0,1,2,3,4,5],[6,7,8,9,10],[11,12,13],[14,15]]
 UNITS_PER_STEP = 1
 UNITS_FREE = 4
-UNITS_SWITCH = 1
+UNITS_SWITCH = 3
 SWITCH_S1V = True
 FIN_LAG = 2
 LN_LAG = 1
 LNW = 4
 V1G = lambda i, c: True
-FG = lambda s: 0 if 64 <= s < 74 else 1
+FG = lambda s: 0 if 60 <= s < 79 else 1
 FV = lambda s: 1
 HG_BUFS = 1
 X_BUFS = 4
@@ -55,7 +55,7 @@ def xe_on_scalar(n):
 
 
 def s1_on_vector(i, m):
-    return (i >= 8 and m == 1) or i >= 14
+    return i >= 12
 
 
 def tile_tnet_t_kernel(tc, x, W_fc, b_fc, W_q, out):
@@ -64,7 +64,7 @@ def tile_tnet_t_kernel(tc, x, W_fc, b_fc, W_q, out):
         const = ctx.enter_context(tc.tile_pool(name="const", bufs=1))
         xpool = ctx.enter_context(tc.tile_pool(name="xpool", bufs=X_BUFS))
         agpool = ctx.enter_context(tc.tile_pool(name="agpool", bufs=2))
-        apool = ctx.enter_context(tc.tile_pool(name="apool", bufs=2))
+        apool = ctx.enter_context(tc.tile_pool(name="apool", bufs=4))
         hpool = ctx.enter_context(tc.tile_pool(name="hpool", bufs=3))
         hgpool = ctx.enter_context(tc.tile_pool(name="hgpool", bufs=HG_BUFS))
         ps_x = ctx.enter_context(tc.psum_pool(name="ps_x", bufs=2))

from contextlib import ExitStack

import concourse.mybir as mybir
from concourse.masks import make_identity

F32 = mybir.dt.float32
BF16 = mybir.dt.bfloat16
U32 = mybir.dt.uint32
U8 = mybir.dt.uint8
FP8X4 = mybir.dt.float8_e4m3fn_x4
ACT = mybir.ActivationFunctionType
ALU = mybir.AluOpType

P = 128
B, NX, NH, NY = 8192, 1024, 512, 256
BLK = 512
NB = B // BLK
T = BLK // P
NT = NB * T
FLOPS = 2 * B * NX * NH + 2 * B * NH * NY

GROUPS = [[0,1,2,3,4,5],[6,7,8,9,10],[11,12,13],[14,15]]
UNITS_PER_STEP = 1
UNITS_FREE = 4
UNITS_SWITCH = 3
SWITCH_S1V = True
FIN_LAG = 2
LN_LAG = 1
LNW = 4
V1G = lambda i, c: True
FG = lambda s: 0 if 60 <= s < 79 else 1
FV = lambda s: 1
HG_BUFS = 1
X_BUFS = 4
WQ_AT = 6
LAG_XE = 1
LAG_QA = 3
LAG_L1 = 7
LAG_S1 = 8
LAG_V1 = 12
LAG_HT = 12
LAG_SQ = 13
LAG_QH = 13
LAG_L2 = 14
LAG_E = 15
LAG_E2 = 16


def dummies(n):
    return 0


def xe_on_scalar(n):
    return False


def s1_on_vector(i, m):
    return i >= 12


def tile_tnet_t_kernel(tc, x, W_fc, b_fc, W_q, out):
    nc = tc.nc
    with ExitStack() as ctx:
        const = ctx.enter_context(tc.tile_pool(name="const", bufs=1))
        xpool = ctx.enter_context(tc.tile_pool(name="xpool", bufs=X_BUFS))
        agpool = ctx.enter_context(tc.tile_pool(name="agpool", bufs=2))
        apool = ctx.enter_context(tc.tile_pool(name="apool", bufs=4))
        hpool = ctx.enter_context(tc.tile_pool(name="hpool", bufs=3))
        hgpool = ctx.enter_context(tc.tile_pool(name="hgpool", bufs=HG_BUFS))
        ps_x = ctx.enter_context(tc.psum_pool(name="ps_x", bufs=2))
        ps_h = ctx.enter_context(tc.psum_pool(name="ps_h", bufs=2))
        ps_z = ctx.enter_context(tc.psum_pool(name="ps_z", bufs=2))
        ps_g = ctx.enter_context(tc.psum_pool(name="ps_g", bufs=2))
        ctx.enter_context(tc.manual_schedule())

        ident = const.tile([P, P], F32, name="ident")
        wfc_sb = const.tile([P, 4, NX], BF16, name="wfc_sb")
        wg = const.tile([P, 2 * NH * 4], BF16, name="wg", align_bytes=64)
        wfc_codes = const.tile([P, 2, NH], U32, name="wfc_codes", align_bytes=64)
        wfc_scales = const.tile([P, 2, NH], U8, name="wfc_scales", align_bytes=64)
        b_bf = const.tile([P, 4], BF16, name="b_bf")
        bias = const.tile([P, 4], F32, name="bias")
        wq_sb = const.tile([P, 2, NH], BF16, name="wq_sb")
        wqg = const.tile([P, NY * 4], BF16, name="wqg", align_bytes=64)
        wq_codes = const.tile([P, NY], U32, name="wq_codes", align_bytes=64)
        wq_scales = const.tile([P, NY], U8, name="wq_scales", align_bytes=64)
        ww = const.tile([P, 2], F32, name="ww")
        wwb1 = const.tile([P, NY], F32, name="wwb1")
        junk_sq = const.tile([P, NH], BF16, name="junk_sq")
        junk_ex = const.tile([P, NY], BF16, name="junk_ex")
        hh = const.tile([P, NT], F32, name="hh")
        umin = const.tile([P, NT], F32, name="umin")
        lmin = const.tile([P, NT], F32, name="lmin")
        shift = const.tile([P, NT], F32, name="shift")
        ssum = const.tile([P, NT], F32, name="ssum")
        lns = const.tile([P, NT], F32, name="lns")
        u_tiles = [const.tile([P, T, NY], F32, name="u%d" % i) for i in range(NB)]

        xs = {}
        xts = {}
        agt = {}
        a_codes = {}
        a_scales = {}
        zs = {}
        h32 = {}
        hgp = {}
        h_codes = {}
        h_scales = {}
        hts = {}
        gps = {}
        wq_tmp = {}

        def load(i, pieces):
            if pieces[0] == 0:
                xs[i] = xpool.tile([P, T, NX], BF16, name="x%d" % i, tag="x")
            src = x[i * BLK:(i + 1) * BLK, :].rearrange("(p t) k -> p t k", t=T)
            t0, t1 = pieces
            nc.sync.dma_start(out=xs[i][:, t0:t1, :], in_=src[:, t0:t1, :])

        def load_wfc(m):
            nc.sync.dma_start(
                out=wfc_sb[:, m, :], in_=W_fc.rearrange("(p m) k -> p m k", m=4)[:, m, :]
            )

        wts = {}

        def wfc_pe(m):
            wt = ps_h.tile([P, 512], F32, name="wt%d" % m, tag="ht")
            wts[m] = wt
            words = wfc_sb[:, m, :].bitcast(F32)
            for gu in range(4):
                nc.tensor.transpose(
                    wt[:, gu * P:(gu + 1) * P], words[:, gu * P:(gu + 1) * P], ident[:]
                )

        def wfc_exit(m):
            dst = wg[:].bitcast(F32).rearrange("p (g c u) -> p g c u", g=2, u=2)
            nc.scalar.copy(
                out=dst[:, :, m * P:(m + 1) * P, :],
                in_=wts[m][:].rearrange("p (g u n) -> p g n u", g=2, u=2),
            )

        def wfc_quant(m):
            for g in range(2):
                c0 = g * NH + m * P
                nc.vector.quantize_mx(
                    out=wfc_codes[:, g, m * P:(m + 1) * P].bitcast(FP8X4),
                    scales=wfc_scales[:, g, m * P:(m + 1) * P],
                    in_=wg[:, c0 * 4:(c0 + P) * 4],
                )

        def setup_wq(phase):
            if phase == 0:
                for c in range(2):
                    nc.scalar.activation(
                        out=junk_sq[:], in_=wq_sb[:, c, :], func=ACT.Square,
                        accum_out=ww[:, c:c + 1],
                    )
                wqt = ps_h.tile([P, 512], F32, name="wqt", tag="ht")
                wq_tmp["wqt"] = wqt
                for c in range(2):
                    words = wq_sb[:, c, :].bitcast(F32).rearrange("j (p u) -> j u p", u=2)
                    for u in range(2):
                        nc.tensor.transpose(
                            wqt[:, u * NY + c * P:u * NY + (c + 1) * P], words[:, u, :], ident[:]
                        )
            elif phase == 1:
                wwps = ps_g.tile([P, NY], F32, name="wwps", tag="g")
                wq_tmp["wwps"] = wwps
                for c in range(2):
                    rep = const.tile([P, P], F32, name="rep%d" % c)
                    nc.vector.tensor_copy(out=rep[:], in_=ww[:, c:c + 1].to_broadcast([P, P]))
                    nc.tensor.transpose(wwps[:, c * P:(c + 1) * P], rep[:], ident[:])
                nc.vector.tensor_scalar(
                    out=wqg[:].rearrange("p (j u e) -> p j u e", u=2, e=2),
                    in0=wq_tmp["wqt"][:].bitcast(BF16).rearrange("p (u j e) -> p j u e", u=2, e=2),
                    scalar1=-2.0, scalar2=None, op0=ALU.mult,
                )
            else:
                nc.vector.tensor_scalar(
                    out=wwb1[:], in0=wq_tmp["wwps"][:], scalar1=1.0, scalar2=None, op0=ALU.add
                )
                nc.vector.quantize_mx(
                    out=wq_codes[:].bitcast(FP8X4), scales=wq_scales[:], in_=wqg[:]
                )

        def xt_pe(n):
            i, t = n // T, n % T
            xt = ps_x.tile([P, 512], F32, name="xt%d" % n, tag="xt")
            xts[n] = xt
            words = xs[i][:, t, :].bitcast(F32)
            for g in range(2):
                for u in range(2):
                    nc.tensor.transpose(
                        xt[:, (u * 2 + g) * P:(u * 2 + g + 1) * P],
                        words[:, (g * 2 + u) * P:(g * 2 + u + 1) * P],
                        ident[:],
                    )

        def l1_pe(n):
            i, m = n // T, n % T
            z = ps_z.tile([P, BLK], F32, name="z%d" % n, tag="z")
            zs[n] = z
            passes = [(0, True, True)] * dummies(n) + [(0, True, False), (1, False, True)]
            for g, first, last in passes:
                nc.tensor.matmul_mx(
                    out=z[:],
                    lhsT=wfc_codes[:, g, m * P:(m + 1) * P].bitcast(FP8X4),
                    lhsT_scale=wfc_scales[:, g, m * P:(m + 1) * P],
                    rhs=a_codes[i][:, g, :].bitcast(FP8X4),
                    rhs_scale=a_scales[i][:, g, :],
                    start=first, stop=last,
                )

        def ht_pe(n):
            i, t = n // T, n % T
            ht = ps_h.tile([P, 512], F32, name="ht%d" % n, tag="ht")
            hts[n] = ht
            for m in range(4):
                nc.tensor.transpose(
                    ht[:, m * P:(m + 1) * P], h32[i][:, m, t * P:(t + 1) * P], ident[:]
                )

        def l2_pe(n):
            i, t = n // T, n % T
            gp = ps_g.tile([P, NY], F32, name="g%d" % n, tag="g")
            gps[n] = gp
            nc.tensor.matmul_mx(
                out=gp[:],
                lhsT=h_codes[i][:, t * P:(t + 1) * P].bitcast(FP8X4),
                lhsT_scale=h_scales[i][:, t * P:(t + 1) * P],
                rhs=wq_codes[:].bitcast(FP8X4),
                rhs_scale=wq_scales[:],
                start=True, stop=True,
            )

        def xe(n):
            if n % 2 == 0:
                agt[n // 2] = agpool.tile(
                    [P, 2, 2, P, 4], BF16, name="ag%d" % n, tag="ag", align_bytes=64
                )
            dst = agt[n // 2][:, :, n % 2, :, :].rearrange("p g r (u e) -> p g r u e", u=2)
            src = xts[n][:].bitcast(BF16).rearrange("p (u g r e) -> p g r u e", u=2, g=2, e=2)
            if xe_on_scalar(n):
                nc.scalar.activation(out=dst, in_=src, func=ACT.Relu)
            else:
                nc.vector.tensor_scalar(out=dst, in0=src, scalar1=0.0, scalar2=None, op0=ALU.max)

        def qa(n):
            pair, g = n // 2, n % 2
            i, t = n // T, n % T
            if t == 0:
                a_codes[i] = apool.tile([P, 2, BLK], U32, name="ac%d" % i, tag="ac", align_bytes=64)
                a_scales[i] = apool.tile([P, 2, BLK], U8, name="as%d" % i, tag="as", align_bytes=64)
            c0 = (pair % 2) * 2 * P
            nc.vector.quantize_mx(
                out=a_codes[i][:, g, c0:c0 + 2 * P].bitcast(FP8X4),
                scales=a_scales[i][:, g, c0:c0 + 2 * P],
                in_=agt[pair][:, g, :, :, :].rearrange("p t r f -> p (t r f)"),
            )

        def s1(n):
            i, m = n // T, n % T
            if m == 0:
                h32[i] = hpool.tile([P, 4, BLK], F32, name="h32_%d" % i, tag="h32")
            state["s1v"] = s1_on_vector(i, m) or (SWITCH_S1V and next_unit_switches())
            if state["s1v"]:
                nc.vector.tensor_scalar(
                    out=h32[i][:, m, :], in0=zs[n][:], scalar1=bias[:, m:m + 1], scalar2=0.0,
                    op0=ALU.add, op1=ALU.max,
                )
            else:
                nc.scalar.activation(
                    out=h32[i][:, m, :], in_=zs[n][:], func=ACT.Relu, bias=bias[:, m:m + 1],
                    scale=1.0,
                )

        def v1(n):
            i, c = n // T, n % T
            hgp[n] = hgpool.tile([P, P, 4], BF16, name="hg%d" % n, tag="hg", align_bytes=64)
            src = h32[i][:, :, c * P:(c + 1) * P].rearrange("p m b -> p b m")
            if V1G(i, c):
                nc.gpsimd.tensor_scalar(
                    out=hgp[n][:], in0=src, scalar1=1.0, scalar2=0.0, op0=ALU.mult, op1=ALU.add
                )
            else:
                nc.vector.tensor_copy(out=hgp[n][:], in_=src)

        def qh(n):
            i, c = n // T, n % T
            if c == 0:
                h_codes[i] = hpool.tile([P, BLK], U32, name="hc%d" % i, tag="hc", align_bytes=64)
                h_scales[i] = hpool.tile([P, BLK], U8, name="hs%d" % i, tag="hs", align_bytes=64)
            nc.vector.quantize_mx(
                out=h_codes[i][:, c * P:(c + 1) * P].bitcast(FP8X4),
                scales=h_scales[i][:, c * P:(c + 1) * P],
                in_=hgp[n][:].rearrange("p b m -> p (b m)"),
            )

        def sq(n):
            nc.scalar.activation(
                out=junk_sq[:], in_=hts[n][:], func=ACT.Square, accum_out=hh[:, n:n + 1]
            )

        def e1(n):
            i, t = n // T, n % T
            u = u_tiles[i]
            nc.vector.scalar_tensor_tensor(
                out=u[:, t, :], in0=gps[n][:], scalar=hh[:, n:n + 1], in1=wwb1[:],
                op0=ALU.add, op1=ALU.add,
            )

        def e2(n):
            i, t = n // T, n % T
            u = u_tiles[i]
            nc.vector.tensor_scalar(
                out=u[:, t, :], in0=u[:, t, :], scalar1=1.0, scalar2=None,
                op0=ALU.max, op1=ALU.min, accum_out=umin[:, n:n + 1],
            )

        units = []
        for q in range(len(GROUPS)):
            if q > 0:
                units.append(("LS", q - 1, 0))
            for i in GROUPS[q]:
                for t in range(0, T, LNW):
                    units.append(("LN", i, t))
            units.append(("LM", q, 0))
            for i in GROUPS[q]:
                for t in range(T):
                    units.append(("EX", i, t))
        units.append(("LS", len(GROUPS) - 1, 0))
        state = {"unit": 0, "ready": -1, "fin": 0, "table": "", "s1v": False}

        def next_unit_switches():
            if state["unit"] >= len(units):
                return False
            kind, a, t = units[state["unit"]]
            if kind == "LN" and a * T + t + LNW - 1 > state["ready"]:
                return False
            return ("EX" if kind == "EX" else "LN") != state["table"]
        fins = []

        def emit_units(limit):
            n = 0
            while state["unit"] < len(units) and n < limit:
                kind, a, t = units[state["unit"]]
                if kind == "LN" and a * T + t + LNW - 1 > state["ready"]:
                    return
                if kind == "LM":
                    c0 = GROUPS[a][0] * T
                    c1 = (GROUPS[a][-1] + 1) * T
                    nc.scalar.activation(out=lmin[:, c0:c1], in_=umin[:, c0:c1], func=ACT.Ln)
                elif kind == "LS":
                    c0 = GROUPS[a][0] * T
                    c1 = (GROUPS[a][-1] + 1) * T
                    nc.scalar.activation(out=lns[:, c0:c1], in_=ssum[:, c0:c1], func=ACT.Ln)
                    fins.append((a, -1))
                    for i in GROUPS[a]:
                        for tt in range(T):
                            fins.append((i, tt))
                else:
                    col = a * T + t
                    u = u_tiles[a]
                    if kind == "LN":
                        nc.scalar.activation(
                            out=u[:, t:t + LNW, :], in_=u[:, t:t + LNW, :], func=ACT.Ln
                        )
                        n += LNW - 1
                    else:
                        nc.scalar.activation(
                            out=junk_ex[:], in_=u[:, t, :], func=ACT.Exp, scale=-1.0,
                            bias=lmin[:, col:col + 1], accum_out=ssum[:, col:col + 1],
                        )
                state["table"] = "EX" if kind == "EX" else "LN"
                state["unit"] += 1
                n += 1

        def emit_fins(limit, upto, eng):
            n = 0
            while state["fin"] < min(upto, len(fins)) and n < limit:
                i, t = fins[state["fin"]]
                if t < 0 and eng is not nc.vector:
                    return
                if t < 0:
                    c0 = GROUPS[i][0] * T
                    c1 = (GROUPS[i][-1] + 1) * T
                    nc.vector.tensor_tensor(
                        out=shift[:, c0:c1], in0=lmin[:, c0:c1], in1=lns[:, c0:c1], op=ALU.subtract
                    )
                else:
                    col = i * T + t
                    u = u_tiles[i]
                    eng.tensor_scalar(
                        out=u[:, t, :], in0=u[:, t, :], scalar1=-1.0,
                        scalar2=shift[:, col:col + 1], op0=ALU.mult, op1=ALU.add,
                    )
                if t == T - 1:
                    nc.sync.dma_start(
                        out=out[i * BLK:(i + 1) * BLK, :].rearrange("(p t) j -> p t j", t=T),
                        in_=u[:],
                    )
                state["fin"] += 1
                n += 1

        def ok(n):
            return 0 <= n < NT

        make_identity(nc, ident[:])
        load(0, (0, 1))
        load(0, (1, 2))
        load_wfc(0)
        load(0, (2, 3))
        load_wfc(1)
        load(0, (3, 4))
        load_wfc(2)
        load_wfc(3)
        load(1, (0, 2))
        load(1, (2, 4))
        nc.scalar.dma_start(out=b_bf[:], in_=b_fc.rearrange("(p m) -> p m", m=4))
        nc.scalar.dma_start(out=wq_sb[:], in_=W_q.rearrange("(c j) k -> j c k", c=2))
        for i in range(2, X_BUFS):
            load(i, (0, T))

        fin_hist = []
        for step in range(NT + LAG_E2 + 1):
            if ok(step):
                xt_pe(step)
            if 0 <= step - 1 < 4:
                wfc_pe(step - 1)
            if 0 <= step - 2 < 4:
                wfc_exit(step - 2)
            if 0 <= step - 3 < 4:
                wfc_quant(step - 3)
            if step == 4:
                nc.vector.tensor_copy(out=bias[:], in_=b_bf[:])
            if ok(step - LAG_HT):
                ht_pe(step - LAG_HT)
            if ok(step - LAG_L1):
                l1_pe(step - LAG_L1)
            if ok(step - LAG_L2):
                l2_pe(step - LAG_L2)

            if ok(step - LAG_QA):
                qa(step - LAG_QA)
            if step >= FIN_LAG:
                emit_fins(FV(step), fin_hist[step - FIN_LAG], nc.vector)
            if ok(step - LAG_QH):
                qh(step - LAG_QH)
            if ok(step - LAG_V1):
                v1(step - LAG_V1)
            if step >= FIN_LAG:
                emit_fins(FG(step), fin_hist[step - FIN_LAG], nc.gpsimd)
            if ok(step - LAG_XE):
                xe(step - LAG_XE)
            if ok(step - LAG_E):
                e1(step - LAG_E)
            if ok(step - LAG_SQ):
                sq(step - LAG_SQ)
            if ok(step - LAG_S1):
                s1(step - LAG_S1)
            if ok(step - LAG_E2):
                e2(step - LAG_E2)
            done = step - LAG_E2 - LN_LAG
            state["ready"] = min(NT - 1, done)
            if next_unit_switches():
                emit_units(UNITS_SWITCH)
            elif state["s1v"] or not ok(step - LAG_S1):
                emit_units(UNITS_FREE)
            else:
                emit_units(UNITS_PER_STEP)
            state["s1v"] = False
            fin_hist.append(len(fins))
            if WQ_AT <= step < WQ_AT + 3:
                setup_wq(step - WQ_AT)
            if step % T == T - 1 and step // T + X_BUFS < NB:
                load(step // T + X_BUFS, (0, T))
        state["ready"] = NT - 1
        emit_units(len(units))
        emit_fins(len(fins), len(fins), nc.vector)
